import numpy as np
import ml_dtypes


def mxq(x, axis, fmt="e4m3"):
    dtype, down = {"e4m3": (ml_dtypes.float8_e4m3fn, 7), "e5m2": (ml_dtypes.float8_e5m2, 14)}[fmt]
    v = np.moveaxis(np.asarray(x, np.float32).astype(ml_dtypes.bfloat16).astype(np.float64), axis, -1)
    blocks = v.reshape(v.shape[:-1] + (-1, 32))
    amax = np.abs(blocks).max(-1, keepdims=True)
    byte = np.maximum(np.where(amax > 0, np.frexp(amax)[1] - 1 + 127, 0) - down, 1)
    scale = np.exp2(byte - 127.0)
    codes = (blocks / scale).astype(np.float32).astype(dtype).astype(np.float64)
    return np.moveaxis((codes * scale).reshape(v.shape), -1, axis)


WIDE = False


def mx_kscale(k):
    if not WIDE:
        return np.ones(k)
    levels = np.array([10, -10, 5, -5, 0])
    a = np.random.permutation(np.resize(levels, k // 512 * 4)).reshape(k // 512, 4)
    idx = np.arange(k)
    return np.exp2(a[idx // 512, idx % 128 // 32])


BF16 = ml_dtypes.bfloat16


def bf(x):
    return np.asarray(x, np.float32).astype(BF16)


def f64(x):
    return np.asarray(x).astype(np.float64)


E2M1 = np.array([0.0, 0.5, 1.0, 1.5, 2.0, 3.0, 4.0, 6.0, -0.0, -0.5, -1.0, -1.5, -2.0, -3.0, -4.0, -6.0])


def pack_weight(w, fmt):
    k, n = w.shape
    w = f64(bf(w)).reshape(k // 32, 32, n)
    amax = np.abs(w).max(1)
    if fmt == "e4m3":
        byte = np.frexp(amax)[1] - 1 + 127 - 7
    else:
        mant, ex = np.frexp(amax / 6.0)
        byte = np.where(mant > 0.5, ex, ex - 1) + 127
    byte = np.clip(np.where(amax > 0, byte, 1), 1, 254)
    scaled = (w * np.exp2(127.0 - byte)[:, None, :]).reshape(k, n).astype(np.float32)
    by_word = np.ascontiguousarray(scaled.reshape(k // 512, 128, 4, n).transpose(0, 1, 3, 2))
    if fmt == "e4m3":
        words = by_word.astype(ml_dtypes.float8_e4m3fn).view(np.uint8)
    else:
        c = by_word.astype(ml_dtypes.float4_e2m1fn).view(np.uint8) & 0xF
        words = c[..., 0::2] | (c[..., 1::2] << 4)
    return np.ascontiguousarray(words), np.ascontiguousarray(byte.astype(np.uint8).reshape(k // 512, 16, n))


def unpack_weight(words, scales, fmt):
    g, p, n, _ = words.shape
    if fmt == "e4m3":
        vals = np.ascontiguousarray(words).view(ml_dtypes.float8_e4m3fn).astype(np.float64)
    else:
        nib = np.empty((g, p, n, 4), np.uint8)
        nib[..., 0::2] = words & 0xF
        nib[..., 1::2] = words >> 4
        vals = E2M1[nib]
    vals = vals * np.repeat(np.exp2(scales.astype(np.float64) - 127.0), 8, axis=1)[..., None]
    return vals.transpose(0, 1, 3, 2).reshape(g * 512, n)


G, B, NF, T, I, R, H = 1, 4096, 512, 512, 512, 1024, 256


def setup_inputs():
    kf, kt, kr = mx_kscale(NF), mx_kscale(T), mx_kscale(R)
    v = bf(np.random.standard_normal((B, NF)) * kf)
    s = bf(np.random.standard_normal((B, T)) * kt)
    Ca = np.random.standard_normal((G, NF, R)) / np.sqrt(NF) / kf[:, None] * kr
    Cb = np.random.standard_normal((G, T, R)) / np.sqrt(T) / kt[:, None]
    Cc = np.random.standard_normal((G, R, H)) * 0.7 / np.sqrt(R) / kr[:, None]
    Ca_words, Ca_scales = pack_weight(Ca.reshape(-1, R), "e4m3")
    Cb_words, Cb_scales = pack_weight(Cb.reshape(-1, R), "e4m3")
    Cc_words, Cc_scales = pack_weight(Cc.reshape(-1, H), "e4m3")
    return {"v": v,
            "s": s,
            "Ca_words": Ca_words, "Ca_scales": Ca_scales,
            "Cb_words": Cb_words, "Cb_scales": Cb_scales,
            "Cc_words": Cc_words, "Cc_scales": Cc_scales}


def reference(v, s, Ca_words, Ca_scales, Cb_words, Cb_scales, Cc_words, Cc_scales):
    t3 = mxq(f64(v), 1, "e4m3") @ unpack_weight(Ca_words, Ca_scales, "e4m3").reshape(G, NF, R)
    t4 = mxq(f64(s), 1, "e4m3") @ unpack_weight(Cb_words, Cb_scales, "e4m3").reshape(G, T, R)
    return mxq(t3 * t4, 2, "e4m3") @ unpack_weight(Cc_words, Cc_scales, "e4m3").reshape(G, R, H)

@@ -1,0 +1,198 @@
+from contextlib import ExitStack
+
+import concourse.mybir as mybir
+from concourse.masks import make_identity
+
+BF16 = mybir.dt.bfloat16
+F32 = mybir.dt.float32
+I32 = mybir.dt.int32
+U32 = mybir.dt.uint32
+U8 = mybir.dt.uint8
+FP8X4 = mybir.dt.float8_e4m3fn_x4
+
+P = 128
+PACK = 4
+K_PASS = P * PACK
+HALF = 2
+
+BATCH = 4096
+FEATURES = 512
+RANK = 1024
+HIDDEN = 256
+R_PASSES = RANK // K_PASS
+
+TILES_PER_CHUNK = 4
+CHUNK_ROWS = TILES_PER_CHUNK * P
+N_CHUNKS = BATCH // CHUNK_ROWS
+N_TILES = BATCH // P
+
+FLOPS = 2 * BATCH * (FEATURES * RANK + FEATURES * RANK + RANK * HIDDEN)
+
+
+def tile_vnclcell_pa_t_e_kernel(
+    tc, v, s, Ca_words, Ca_scales, Cb_words, Cb_scales, Cc_words, Cc_scales, out
+):
+    nc = tc.nc
+    with ExitStack() as ctx:
+        ctx.enter_context(tc.manual_schedule())
+        consts = ctx.enter_context(tc.tile_pool(name="consts", bufs=1))
+        rows = ctx.enter_context(tc.tile_pool(name="rows", bufs=N_CHUNKS))
+        stage = ctx.enter_context(tc.tile_pool(name="stage", bufs=2))
+        products = ctx.enter_context(tc.tile_pool(name="products", bufs=4))
+        banks = ctx.enter_context(tc.psum_pool(name="banks", bufs=1))
+
+        ident = consts.tile([P, P], F32, name="ident")
+        make_identity(nc, ident[:])
+
+        ca_codes = consts.tile([P, RANK], U32, name="ca_codes", align_bytes=64)
+        cb_codes = consts.tile([P, RANK], U32, name="cb_codes", align_bytes=64)
+        cc_codes = consts.tile([P, R_PASSES, HIDDEN], U32, name="cc_codes", align_bytes=64)
+        ca_scales = consts.tile([P, RANK], U8, name="ca_scales", align_bytes=64)
+        cb_scales = consts.tile([P, RANK], U8, name="cb_scales", align_bytes=64)
+        cc_scales = consts.tile([P, R_PASSES, HIDDEN], U8, name="cc_scales", align_bytes=64)
+        nc.vector.memset(ca_scales[:].bitcast(I32), 0)
+        nc.vector.memset(cb_scales[:].bitcast(I32), 0)
+        nc.vector.memset(cc_scales[:].bitcast(I32), 0)
+
+        v_rows = []
+        s_rows = []
+
+        def load_rows(c):
+            chunk = slice(c * CHUNK_ROWS, (c + 1) * CHUNK_ROWS)
+            for source, kept, name in ((v, v_rows, "v_rows"), (s, s_rows, "s_rows")):
+                loaded = rows.tile([P, TILES_PER_CHUNK, FEATURES], BF16, name=name)
+                nc.sync.dma_start(
+                    out=loaded[:],
+                    in_=source[chunk, :].rearrange("(p t) k -> p t k", t=TILES_PER_CHUNK),
+                )
+                kept.append(loaded)
+
+        def load_scale_rows(plane, dram_rows_of_quadrant):
+            for quadrant in range(4):
+                nc.sync.dma_start(
+                    out=plane[32 * quadrant : 32 * quadrant + 4].bitcast(I32),
+                    in_=dram_rows_of_quadrant(slice(4 * quadrant, 4 * quadrant + 4)).bitcast(I32),
+                )
+
+        load_rows(0)
+        load_scale_rows(ca_scales, lambda q: Ca_scales[0, q, :])
+        load_scale_rows(cb_scales, lambda q: Cb_scales[0, q, :])
+        nc.sync.dma_start(
+            out=ca_codes[:].bitcast(I32),
+            in_=Ca_words[0].rearrange("p n t -> p (n t)").bitcast(I32),
+        )
+        nc.sync.dma_start(
+            out=cb_codes[:].bitcast(I32),
+            in_=Cb_words[0].rearrange("p n t -> p (n t)").bitcast(I32),
+        )
+        load_scale_rows(cc_scales, lambda q: Cc_scales[:, q, :].rearrange("g q n -> q g n"))
+        nc.sync.dma_start(
+            out=cc_codes[:].bitcast(I32),
+            in_=Cc_words.rearrange("g p n t -> p g (n t)").bitcast(I32),
+        )
+        for c in range(1, N_CHUNKS):
+            load_rows(c)
+
+        def regroup_and_quantise(planes, name):
+            grouped = stage.tile([P, 2, P, PACK], BF16, name=name + "_grouped", align_bytes=64)
+            nc.scalar.copy(
+                out=grouped[:].bitcast(F32), in_=planes[:].rearrange("p a u b -> p a b u")
+            )
+            codes = stage.tile([P, 2, P], U32, name=name + "_codes", align_bytes=64)
+            scales = stage.tile([P, 2, P], U8, name=name + "_scales", align_bytes=64)
+            nc.vector.quantize_mx(
+                out=codes[:].rearrange("p a b -> p (a b)").bitcast(FP8X4),
+                scales=scales[:].rearrange("p a b -> p (a b)"),
+                in_=grouped[:].rearrange("p a b t -> p (a b t)"),
+            )
+            return codes, scales
+
+        quantised_inputs = {}
+        fused = {}
+        quantised_fused = {}
+        results = {}
+
+        def quantise_inputs(i):
+            c, t = divmod(i, TILES_PER_CHUNK)
+            planes = banks.tile([P, 2, HALF, P], F32, name="input_planes")
+            for a, loaded in enumerate((v_rows[c], s_rows[c])):
+                words = loaded[:, t, :].bitcast(F32)
+                for u in range(HALF):
+                    nc.tensor.transpose(
+                        planes[:, a, u, :], words[:, u : FEATURES // 2 : HALF], ident[:]
+                    )
+            quantised_inputs[i] = regroup_and_quantise(planes, "input")
+
+        def first_products(i):
+            codes, scales = quantised_inputs[i]
+            fused_rows = products.tile([P, R_PASSES, HALF, K_PASS // HALF], BF16, name="fused_rows")
+            for g in range(R_PASSES):
+                columns = slice(g * K_PASS, (g + 1) * K_PASS)
+                sums = []
+                for a, (w_codes, w_scales) in enumerate(
+                    ((ca_codes, ca_scales), (cb_codes, cb_scales))
+                ):
+                    acc = banks.tile([P, K_PASS], F32, name="sums_%d_%d" % (a, g))
+                    nc.tensor.matmul_mx(
+                        out=acc[:],
+                        lhsT=codes[:, a, :].bitcast(FP8X4),
+                        lhsT_scale=scales[:, a, :],
+                        rhs=w_codes[:, columns].bitcast(FP8X4),
+                        rhs_scale=w_scales[:, columns],
+                        start=True,
+                        stop=True,
+                    )
+                    sums.append(acc[:].rearrange("b (p u e) -> b u p e", u=HALF, e=2))
+                left = stage.tile([P, HALF, P, 2], F32, name="left")
+                nc.scalar.copy(out=left[:], in_=sums[0])
+                nc.vector.tensor_tensor(
+                    out=fused_rows[:, g].rearrange("b u (p e) -> b u p e", e=2),
+                    in0=sums[1],
+                    in1=left[:],
+                    op=mybir.AluOpType.mult,
+                )
+            fused[i] = fused_rows
+
+        def quantise_fused(i):
+            fused_rows = fused[i]
+            planes = banks.tile([P, R_PASSES, HALF, P], F32, name="fused_planes")
+            for g in range(R_PASSES):
+                for u in range(HALF):
+                    nc.tensor.transpose(
+                        planes[:, g, u, :], fused_rows[:, g, u, :].bitcast(F32), ident[:]
+                    )
+            quantised_fused[i] = regroup_and_quantise(planes, "fused")
+
+        def last_product(i):
+            codes, scales = quantised_fused[i]
+            c, t = divmod(i, TILES_PER_CHUNK)
+            acc = banks.tile([P, HIDDEN], F32, name="out_sums")
+            for g in range(R_PASSES):
+                nc.tensor.matmul_mx(
+                    out=acc[:],
+                    lhsT=codes[:, g, :].bitcast(FP8X4),
+                    lhsT_scale=scales[:, g, :],
+                    rhs=cc_codes[:, g, :].bitcast(FP8X4),
+                    rhs_scale=cc_scales[:, g, :],
+                    start=(g == 0),
+                    stop=(g == R_PASSES - 1),
+                )
+            if t == 0:
+                results[c] = stage.tile([P, TILES_PER_CHUNK, HIDDEN], F32, name="result")
+            nc.vector.tensor_copy(out=results[c][:, t, :], in_=acc[:])
+            if t == TILES_PER_CHUNK - 1:
+                chunk = slice(c * CHUNK_ROWS, (c + 1) * CHUNK_ROWS)
+                nc.sync.dma_start(
+                    out=out[0, chunk, :].rearrange("(p t) h -> p t h", t=TILES_PER_CHUNK),
+                    in_=results[c][:],
+                )
+
+        for step in range(-1, N_TILES + 3):
+            if 0 <= step + 1 < N_TILES:
+                quantise_inputs(step + 1)
+            if 0 <= step - 2 < N_TILES:
+                quantise_fused(step - 2)
+            if 0 <= step - 3 < N_TILES:
+                last_product(step - 3)
+            if 0 <= step < N_TILES:
+                first_products(step)

@@ -21,7 +21,7 @@ RANK = 1024
 HIDDEN = 256
 R_PASSES = RANK // K_PASS
 
-TILES_PER_CHUNK = 4
+TILES_PER_CHUNK = 2
 CHUNK_ROWS = TILES_PER_CHUNK * P
 N_CHUNKS = BATCH // CHUNK_ROWS
 N_TILES = BATCH // P
@@ -39,6 +39,7 @@ def tile_vnclcell_pa_t_e_kernel(
         rows = ctx.enter_context(tc.tile_pool(name="rows", bufs=N_CHUNKS))
         stage = ctx.enter_context(tc.tile_pool(name="stage", bufs=2))
         products = ctx.enter_context(tc.tile_pool(name="products", bufs=4))
+        stores = ctx.enter_context(tc.tile_pool(name="stores", bufs=4))
         banks = ctx.enter_context(tc.psum_pool(name="banks", bufs=1))
 
         ident = consts.tile([P, P], F32, name="ident")
@@ -76,7 +77,6 @@ def tile_vnclcell_pa_t_e_kernel(
 
         load_rows(0)
         load_scale_rows(ca_scales, lambda q: Ca_scales[0, q, :])
-        load_scale_rows(cb_scales, lambda q: Cb_scales[0, q, :])
         nc.sync.dma_start(
             out=ca_codes[:].bitcast(I32),
             in_=Ca_words[0].rearrange("p n t -> p (n t)").bitcast(I32),
@@ -85,12 +85,14 @@ def tile_vnclcell_pa_t_e_kernel(
             out=cb_codes[:].bitcast(I32),
             in_=Cb_words[0].rearrange("p n t -> p (n t)").bitcast(I32),
         )
+        load_scale_rows(cb_scales, lambda q: Cb_scales[0, q, :])
+        load_rows(1)
         load_scale_rows(cc_scales, lambda q: Cc_scales[:, q, :].rearrange("g q n -> q g n"))
         nc.sync.dma_start(
             out=cc_codes[:].bitcast(I32),
             in_=Cc_words.rearrange("g p n t -> p g (n t)").bitcast(I32),
         )
-        for c in range(1, N_CHUNKS):
+        for c in range(2, N_CHUNKS):
             load_rows(c)
 
         def regroup_and_quantise(planes, name):
@@ -178,7 +180,7 @@ def tile_vnclcell_pa_t_e_kernel(
                     stop=(g == R_PASSES - 1),
                 )
             if t == 0:
-                results[c] = stage.tile([P, TILES_PER_CHUNK, HIDDEN], F32, name="result")
+                results[c] = stores.tile([P, TILES_PER_CHUNK, HIDDEN], F32, name="result")
             nc.vector.tensor_copy(out=results[c][:, t, :], in_=acc[:])
             if t == TILES_PER_CHUNK - 1:
                 chunk = slice(c * CHUNK_ROWS, (c + 1) * CHUNK_ROWS)

@@ -37,22 +37,32 @@ def tile_vnclcell_pa_t_e_kernel(
         ctx.enter_context(tc.manual_schedule())
         consts = ctx.enter_context(tc.tile_pool(name="consts", bufs=1))
         rows = ctx.enter_context(tc.tile_pool(name="rows", bufs=N_CHUNKS))
-        stage = ctx.enter_context(tc.tile_pool(name="stage", bufs=2))
-        products = ctx.enter_context(tc.tile_pool(name="products", bufs=4))
+        grouped_pool = ctx.enter_context(tc.tile_pool(name="grouped", bufs=3))
+        operands = ctx.enter_context(tc.tile_pool(name="operands", bufs=4))
+        lefts = ctx.enter_context(tc.tile_pool(name="lefts", bufs=3))
         stores = ctx.enter_context(tc.tile_pool(name="stores", bufs=4))
         banks = ctx.enter_context(tc.psum_pool(name="banks", bufs=1))
 
         ident = consts.tile([P, P], F32, name="ident")
         make_identity(nc, ident[:])
 
-        ca_codes = consts.tile([P, RANK], U32, name="ca_codes", align_bytes=64)
-        cb_codes = consts.tile([P, RANK], U32, name="cb_codes", align_bytes=64)
+        raw_codes = {}
+        raw_scales = {}
+        sorted_codes = {}
+        sorted_scales = {}
+        for w in ("a", "b"):
+            raw_codes[w] = consts.tile([P, RANK], U32, name="raw_codes_" + w, align_bytes=64)
+            raw_scales[w] = consts.tile([P, RANK], U8, name="raw_scales_" + w, align_bytes=64)
+            sorted_codes[w] = consts.tile(
+                [P, R_PASSES, PACK, P], U32, name="sorted_codes_" + w, align_bytes=64
+            )
+            sorted_scales[w] = consts.tile(
+                [P, R_PASSES, PACK, P], U8, name="sorted_scales_" + w, align_bytes=64
+            )
         cc_codes = consts.tile([P, R_PASSES, HIDDEN], U32, name="cc_codes", align_bytes=64)
-        ca_scales = consts.tile([P, RANK], U8, name="ca_scales", align_bytes=64)
-        cb_scales = consts.tile([P, RANK], U8, name="cb_scales", align_bytes=64)
         cc_scales = consts.tile([P, R_PASSES, HIDDEN], U8, name="cc_scales", align_bytes=64)
-        nc.vector.memset(ca_scales[:].bitcast(I32), 0)
-        nc.vector.memset(cb_scales[:].bitcast(I32), 0)
+        nc.vector.memset(raw_scales["a"][:].bitcast(I32), 0)
+        nc.vector.memset(raw_scales["b"][:].bitcast(I32), 0)
         nc.vector.memset(cc_scales[:].bitcast(I32), 0)
 
         v_rows = []
@@ -75,17 +85,21 @@ def tile_vnclcell_pa_t_e_kernel(
                     in_=dram_rows_of_quadrant(slice(4 * quadrant, 4 * quadrant + 4)).bitcast(I32),
                 )
 
+        def load_codes(w, words, g):
+            nc.sync.dma_start(
+                out=raw_codes[w][:, g * K_PASS : (g + 1) * K_PASS].bitcast(I32),
+                in_=words[0]
+                .rearrange("p n t -> p (n t)")[:, g * K_PASS * PACK : (g + 1) * K_PASS * PACK]
+                .bitcast(I32),
+            )
+
         load_rows(0)
-        load_scale_rows(ca_scales, lambda q: Ca_scales[0, q, :])
-        nc.sync.dma_start(
-            out=ca_codes[:].bitcast(I32),
-            in_=Ca_words[0].rearrange("p n t -> p (n t)").bitcast(I32),
-        )
-        nc.sync.dma_start(
-            out=cb_codes[:].bitcast(I32),
-            in_=Cb_words[0].rearrange("p n t -> p (n t)").bitcast(I32),
-        )
-        load_scale_rows(cb_scales, lambda q: Cb_scales[0, q, :])
+        load_scale_rows(raw_scales["a"], lambda q: Ca_scales[0, q, :])
+        load_codes("a", Ca_words, 0)
+        load_codes("b", Cb_words, 0)
+        load_scale_rows(raw_scales["b"], lambda q: Cb_scales[0, q, :])
+        load_codes("a", Ca_words, 1)
+        load_codes("b", Cb_words, 1)
         load_rows(1)
         load_scale_rows(cc_scales, lambda q: Cc_scales[:, q, :].rearrange("g q n -> q g n"))
         nc.sync.dma_start(
@@ -95,13 +109,55 @@ def tile_vnclcell_pa_t_e_kernel(
         for c in range(2, N_CHUNKS):
             load_rows(c)
 
-        def regroup_and_quantise(planes, name):
-            grouped = stage.tile([P, 2, P, PACK], BF16, name=name + "_grouped", align_bytes=64)
-            nc.scalar.copy(
-                out=grouped[:].bitcast(F32), in_=planes[:].rearrange("p a u b -> p a b u")
+        def sort_columns(w, g):
+            columns = slice(g * K_PASS, (g + 1) * K_PASS)
+            nc.vector.tensor_copy(
+                out=sorted_codes[w][:, g].bitcast(I32),
+                in_=raw_codes[w][:, columns].bitcast(I32).rearrange("p (m t) -> p t m", t=PACK),
             )
-            codes = stage.tile([P, 2, P], U32, name=name + "_codes", align_bytes=64)
-            scales = stage.tile([P, 2, P], U8, name=name + "_scales", align_bytes=64)
+            nc.vector.tensor_copy(
+                out=sorted_scales[w][:, g],
+                in_=raw_scales[w][:, columns].rearrange("p (m t) -> p t m", t=PACK),
+            )
+
+        planes_of = {}
+        grouped_of = {}
+        inputs_of = {}
+        sums_of = {}
+        left_of = {}
+        fused_of = {}
+        fused_codes_of = {}
+        out_sums_of = {}
+        results = {}
+
+        def live(i):
+            return 0 <= i < N_TILES
+
+        def transpose_inputs(i):
+            if not live(i):
+                return
+            c, t = divmod(i, TILES_PER_CHUNK)
+            planes = banks.tile([P, 2, HALF, P], F32, name="planes_%d" % (i % 2))
+            for a, loaded in enumerate((v_rows[c], s_rows[c])):
+                words = loaded[:, t, :].bitcast(F32)
+                for u in range(HALF):
+                    nc.tensor.transpose(
+                        planes[:, a, u, :], words[:, u : FEATURES // 2 : HALF], ident[:]
+                    )
+            planes_of[i] = planes
+
+        def copy_inputs(i):
+            if not live(i):
+                return
+            grouped = grouped_pool.tile([P, 2, P, PACK], BF16, name="in_grouped", align_bytes=64)
+            nc.scalar.copy(
+                out=grouped[:].bitcast(F32), in_=planes_of[i][:].rearrange("p a u b -> p a b u")
+            )
+            grouped_of[i] = grouped
+
+        def quantise(grouped, name):
+            codes = operands.tile([P, 2, P], U32, name=name + "_codes", align_bytes=64)
+            scales = operands.tile([P, 2, P], U8, name=name + "_scales", align_bytes=64)
             nc.vector.quantize_mx(
                 out=codes[:].rearrange("p a b -> p (a b)").bitcast(FP8X4),
                 scales=scales[:].rearrange("p a b -> p (a b)"),
@@ -109,66 +165,58 @@ def tile_vnclcell_pa_t_e_kernel(
             )
             return codes, scales
 
-        quantised_inputs = {}
-        fused = {}
-        quantised_fused = {}
-        results = {}
-
         def quantise_inputs(i):
-            c, t = divmod(i, TILES_PER_CHUNK)
-            planes = banks.tile([P, 2, HALF, P], F32, name="input_planes")
-            for a, loaded in enumerate((v_rows[c], s_rows[c])):
-                words = loaded[:, t, :].bitcast(F32)
-                for u in range(HALF):
-                    nc.tensor.transpose(
-                        planes[:, a, u, :], words[:, u : FEATURES // 2 : HALF], ident[:]
-                    )
-            quantised_inputs[i] = regroup_and_quantise(planes, "input")
+            if live(i):
+                inputs_of[i] = quantise(grouped_of[i], "in")
 
-        def first_products(i):
-            codes, scales = quantised_inputs[i]
-            fused_rows = products.tile([P, R_PASSES, HALF, K_PASS // HALF], BF16, name="fused_rows")
-            for g in range(R_PASSES):
-                columns = slice(g * K_PASS, (g + 1) * K_PASS)
-                sums = []
-                for a, (w_codes, w_scales) in enumerate(
-                    ((ca_codes, ca_scales), (cb_codes, cb_scales))
-                ):
-                    acc = banks.tile([P, K_PASS], F32, name="sums_%d_%d" % (a, g))
+        def first_products(i, g):
+            if not live(i):
+                return
+            codes, scales = inputs_of[i]
+            for a, w in enumerate(("a", "b")):
+                sums = banks.tile([P, PACK, P], F32, name="sums_%s_%d" % (w, g))
+                for t in range(PACK):
                     nc.tensor.matmul_mx(
-                        out=acc[:],
-                        lhsT=codes[:, a, :].bitcast(FP8X4),
-                        lhsT_scale=scales[:, a, :],
-                        rhs=w_codes[:, columns].bitcast(FP8X4),
-                        rhs_scale=w_scales[:, columns],
+                        out=sums[:, t, :],
+                        lhsT=sorted_codes[w][:, g, t, :].bitcast(FP8X4),
+                        lhsT_scale=sorted_scales[w][:, g, t, :],
+                        rhs=codes[:, a, :].bitcast(FP8X4),
+                        rhs_scale=scales[:, a, :],
                         start=True,
                         stop=True,
                     )
-                    sums.append(acc[:].rearrange("b (p u e) -> b u p e", u=HALF, e=2))
-                left = stage.tile([P, HALF, P, 2], F32, name="left")
-                nc.scalar.copy(out=left[:], in_=sums[0])
-                nc.vector.tensor_tensor(
-                    out=fused_rows[:, g].rearrange("b u (p e) -> b u p e", e=2),
-                    in0=sums[1],
-                    in1=left[:],
-                    op=mybir.AluOpType.mult,
+                sums_of[(i, g, w)] = sums
+
+        def copy_left(i, g):
+            if not live(i):
+                return
+            left = lefts.tile([P, P, PACK], F32, name="left")
+            nc.scalar.copy(out=left[:], in_=sums_of[(i, g, "a")][:].rearrange("p t b -> p b t"))
+            left_of[(i, g)] = left
+
+        def multiply(i, g):
+            if not live(i):
+                return
+            if g == 0:
+                fused_of[i] = grouped_pool.tile(
+                    [P, R_PASSES, P, PACK], BF16, name="fused_grouped", align_bytes=64
                 )
-            fused[i] = fused_rows
+            nc.vector.tensor_tensor(
+                out=fused_of[i][:, g],
+                in0=sums_of[(i, g, "b")][:].rearrange("p t b -> p b t"),
+                in1=left_of[(i, g)][:],
+                op=mybir.AluOpType.mult,
+            )
 
         def quantise_fused(i):
-            fused_rows = fused[i]
-            planes = banks.tile([P, R_PASSES, HALF, P], F32, name="fused_planes")
-            for g in range(R_PASSES):
-                for u in range(HALF):
-                    nc.tensor.transpose(
-                        planes[:, g, u, :], fused_rows[:, g, u, :].bitcast(F32), ident[:]
-                    )
-            quantised_fused[i] = regroup_and_quantise(planes, "fused")
+            if live(i):
+                fused_codes_of[i] = quantise(fused_of[i], "fused")
 
         def last_product(i):
-            codes, scales = quantised_fused[i]
-            c, t = divmod(i, TILES_PER_CHUNK)
-            acc = banks.tile([P, HIDDEN], F32, name="out_sums")
+            if not live(i):
+                return
+            codes, scales = fused_codes_of[i]
+            acc = banks.tile([P, HIDDEN], F32, name="out_sums_%d" % (i % 2))
             for g in range(R_PASSES):
                 nc.tensor.matmul_mx(
                     out=acc[:],
@@ -179,22 +227,57 @@ def tile_vnclcell_pa_t_e_kernel(
                     start=(g == 0),
                     stop=(g == R_PASSES - 1),
                 )
+            out_sums_of[i] = acc
+
+        def copy_out(i):
+            if not live(i):
+                return
+            c, t = divmod(i, TILES_PER_CHUNK)
             if t == 0:
                 results[c] = stores.tile([P, TILES_PER_CHUNK, HIDDEN], F32, name="result")
-            nc.vector.tensor_copy(out=results[c][:, t, :], in_=acc[:])
-            if t == TILES_PER_CHUNK - 1:
+                nc.vector.tensor_copy(out=results[c][:, t, :], in_=out_sums_of[i][:])
+            else:
+                nc.scalar.copy(out=results[c][:, t, :], in_=out_sums_of[i][:])
                 chunk = slice(c * CHUNK_ROWS, (c + 1) * CHUNK_ROWS)
                 nc.sync.dma_start(
                     out=out[0, chunk, :].rearrange("(p t) h -> p t h", t=TILES_PER_CHUNK),
                     in_=results[c][:],
                 )
 
-        for step in range(-1, N_TILES + 3):
-            if 0 <= step + 1 < N_TILES:
-                quantise_inputs(step + 1)
-            if 0 <= step - 2 < N_TILES:
-                quantise_fused(step - 2)
-            if 0 <= step - 3 < N_TILES:
-                last_product(step - 3)
-            if 0 <= step < N_TILES:
-                first_products(step)
+        transpose_inputs(0)
+        transpose_inputs(1)
+        copy_inputs(0)
+        copy_inputs(1)
+        sort_columns("a", 0)
+        quantise_inputs(0)
+        sort_columns("b", 0)
+        sort_columns("a", 1)
+        sort_columns("b", 1)
+        quantise_inputs(1)
+
+        for e in range(0, N_TILES + 2, 2):
+            o = e + 1
+            transpose_inputs(e + 2)
+            transpose_inputs(e + 3)
+            copy_inputs(e + 2)
+            copy_inputs(e + 3)
+            quantise_inputs(e + 2)
+            quantise_fused(e - 1)
+            quantise_inputs(e + 3)
+            last_product(e - 2)
+            copy_out(e - 2)
+            first_products(e, 0)
+            copy_left(e, 0)
+            first_products(e, 1)
+            copy_left(e, 1)
+            last_product(e - 1)
+            copy_out(e - 1)
+            multiply(e, 0)
+            multiply(e, 1)
+            first_products(o, 0)
+            copy_left(o, 0)
+            first_products(o, 1)
+            copy_left(o, 1)
+            multiply(o, 0)
+            quantise_fused(e)
+            multiply(o, 1)

@@ -39,9 +39,9 @@ def tile_vnclcell_pa_t_e_kernel(
         rows = ctx.enter_context(tc.tile_pool(name="rows", bufs=N_CHUNKS))
         grouped_pool = ctx.enter_context(tc.tile_pool(name="grouped", bufs=3))
         operands = ctx.enter_context(tc.tile_pool(name="operands", bufs=4))
-        lefts = ctx.enter_context(tc.tile_pool(name="lefts", bufs=3))
+        lefts = ctx.enter_context(tc.tile_pool(name="lefts", bufs=6))
         stores = ctx.enter_context(tc.tile_pool(name="stores", bufs=4))
-        banks = ctx.enter_context(tc.psum_pool(name="banks", bufs=1))
+        banks = ctx.enter_context(tc.psum_pool(name="banks", bufs=8))
 
         ident = consts.tile([P, P], F32, name="ident")
         make_identity(nc, ident[:])
@@ -96,11 +96,11 @@ def tile_vnclcell_pa_t_e_kernel(
         load_rows(0)
         load_scale_rows(raw_scales["a"], lambda q: Ca_scales[0, q, :])
         load_codes("a", Ca_words, 0)
-        load_codes("b", Cb_words, 0)
-        load_scale_rows(raw_scales["b"], lambda q: Cb_scales[0, q, :])
         load_codes("a", Ca_words, 1)
-        load_codes("b", Cb_words, 1)
         load_rows(1)
+        load_scale_rows(raw_scales["b"], lambda q: Cb_scales[0, q, :])
+        load_codes("b", Cb_words, 0)
+        load_codes("b", Cb_words, 1)
         load_scale_rows(cc_scales, lambda q: Cc_scales[:, q, :].rearrange("g q n -> q g n"))
         nc.sync.dma_start(
             out=cc_codes[:].bitcast(I32),
@@ -137,7 +137,7 @@ def tile_vnclcell_pa_t_e_kernel(
             if not live(i):
                 return
             c, t = divmod(i, TILES_PER_CHUNK)
-            planes = banks.tile([P, 2, HALF, P], F32, name="planes_%d" % (i % 2))
+            planes = banks.tile([P, 2, HALF, P], F32, name="bank")
             for a, loaded in enumerate((v_rows[c], s_rows[c])):
                 words = loaded[:, t, :].bitcast(F32)
                 for u in range(HALF):
@@ -149,39 +149,44 @@ def tile_vnclcell_pa_t_e_kernel(
         def copy_inputs(i):
             if not live(i):
                 return
-            grouped = grouped_pool.tile([P, 2, P, PACK], BF16, name="in_grouped", align_bytes=64)
+            c, t = divmod(i, 2)
+            if t == 0:
+                grouped_of[c] = grouped_pool.tile(
+                    [P, 2, 2, P, PACK], BF16, name="in_grouped", align_bytes=64
+                )
             nc.scalar.copy(
-                out=grouped[:].bitcast(F32), in_=planes_of[i][:].rearrange("p a u b -> p a b u")
+                out=grouped_of[c][:, t].bitcast(F32),
+                in_=planes_of[i][:].rearrange("p a u b -> p a b u"),
             )
-            grouped_of[i] = grouped
 
-        def quantise(grouped, name):
-            codes = operands.tile([P, 2, P], U32, name=name + "_codes", align_bytes=64)
-            scales = operands.tile([P, 2, P], U8, name=name + "_scales", align_bytes=64)
+        def quantise_pair(grouped, name):
+            codes = operands.tile([P, 2, 2, P], U32, name=name + "_codes", align_bytes=64)
+            scales = operands.tile([P, 2, 2, P], U8, name=name + "_scales", align_bytes=64)
             nc.vector.quantize_mx(
-                out=codes[:].rearrange("p a b -> p (a b)").bitcast(FP8X4),
-                scales=scales[:].rearrange("p a b -> p (a b)"),
-                in_=grouped[:].rearrange("p a b t -> p (a b t)"),
+                out=codes[:].rearrange("p i a b -> p (i a b)").bitcast(FP8X4),
+                scales=scales[:].rearrange("p i a b -> p (i a b)"),
+                in_=grouped[:].rearrange("p i a b t -> p (i a b t)"),
             )
             return codes, scales
 
-        def quantise_inputs(i):
-            if live(i):
-                inputs_of[i] = quantise(grouped_of[i], "in")
+        def quantise_inputs(c):
+            if live(2 * c):
+                inputs_of[c] = quantise_pair(grouped_of[c], "in")
 
-        def first_products(i, g):
+        def first_products(i, a):
             if not live(i):
                 return
-            codes, scales = inputs_of[i]
-            for a, w in enumerate(("a", "b")):
-                sums = banks.tile([P, PACK, P], F32, name="sums_%s_%d" % (w, g))
+            codes, scales = inputs_of[i // 2]
+            w = "ab"[a]
+            for g in range(R_PASSES):
+                sums = banks.tile([P, PACK, P], F32, name="bank")
                 for t in range(PACK):
                     nc.tensor.matmul_mx(
                         out=sums[:, t, :],
                         lhsT=sorted_codes[w][:, g, t, :].bitcast(FP8X4),
                         lhsT_scale=sorted_scales[w][:, g, t, :],
-                        rhs=codes[:, a, :].bitcast(FP8X4),
-                        rhs_scale=scales[:, a, :],
+                        rhs=codes[:, i % 2, a, :].bitcast(FP8X4),
+                        rhs_scale=scales[:, i % 2, a, :],
                         start=True,
                         stop=True,
                     )
@@ -197,31 +202,32 @@ def tile_vnclcell_pa_t_e_kernel(
         def multiply(i, g):
             if not live(i):
                 return
-            if g == 0:
-                fused_of[i] = grouped_pool.tile(
-                    [P, R_PASSES, P, PACK], BF16, name="fused_grouped", align_bytes=64
+            c, t = divmod(i, 2)
+            if t == 0 and g == 0:
+                fused_of[c] = grouped_pool.tile(
+                    [P, 2, R_PASSES, P, PACK], BF16, name="fused_grouped", align_bytes=64
                 )
             nc.vector.tensor_tensor(
-                out=fused_of[i][:, g],
+                out=fused_of[c][:, t, g],
                 in0=sums_of[(i, g, "b")][:].rearrange("p t b -> p b t"),
                 in1=left_of[(i, g)][:],
                 op=mybir.AluOpType.mult,
             )
 
-        def quantise_fused(i):
-            if live(i):
-                fused_codes_of[i] = quantise(fused_of[i], "fused")
+        def quantise_fused(c):
+            if live(2 * c):
+                fused_codes_of[c] = quantise_pair(fused_of[c], "fused")
 
         def last_product(i):
             if not live(i):
                 return
-            codes, scales = fused_codes_of[i]
-            acc = banks.tile([P, HIDDEN], F32, name="out_sums_%d" % (i % 2))
+            codes, scales = fused_codes_of[i // 2]
+            acc = banks.tile([P, HIDDEN], F32, name="bank")
             for g in range(R_PASSES):
                 nc.tensor.matmul_mx(
                     out=acc[:],
-                    lhsT=codes[:, g, :].bitcast(FP8X4),
-                    lhsT_scale=scales[:, g, :],
+                    lhsT=codes[:, i % 2, g, :].bitcast(FP8X4),
+                    lhsT_scale=scales[:, i % 2, g, :],
                     rhs=cc_codes[:, g, :].bitcast(FP8X4),
                     rhs_scale=cc_scales[:, g, :],
                     start=(g == 0),
@@ -235,49 +241,43 @@ def tile_vnclcell_pa_t_e_kernel(
             c, t = divmod(i, TILES_PER_CHUNK)
             if t == 0:
                 results[c] = stores.tile([P, TILES_PER_CHUNK, HIDDEN], F32, name="result")
+            if i % 4 == 3:
                 nc.vector.tensor_copy(out=results[c][:, t, :], in_=out_sums_of[i][:])
             else:
                 nc.scalar.copy(out=results[c][:, t, :], in_=out_sums_of[i][:])
+            if t == TILES_PER_CHUNK - 1:
                 chunk = slice(c * CHUNK_ROWS, (c + 1) * CHUNK_ROWS)
                 nc.sync.dma_start(
                     out=out[0, chunk, :].rearrange("(p t) h -> p t h", t=TILES_PER_CHUNK),
                     in_=results[c][:],
                 )
 
-        transpose_inputs(0)
-        transpose_inputs(1)
-        copy_inputs(0)
-        copy_inputs(1)
-        sort_columns("a", 0)
-        quantise_inputs(0)
-        sort_columns("b", 0)
-        sort_columns("a", 1)
-        sort_columns("b", 1)
-        quantise_inputs(1)
-
-        for e in range(0, N_TILES + 2, 2):
-            o = e + 1
-            transpose_inputs(e + 2)
-            transpose_inputs(e + 3)
-            copy_inputs(e + 2)
-            copy_inputs(e + 3)
-            quantise_inputs(e + 2)
-            quantise_fused(e - 1)
-            quantise_inputs(e + 3)
-            last_product(e - 2)
-            copy_out(e - 2)
-            first_products(e, 0)
-            copy_left(e, 0)
+        for e in range(-4, N_TILES + 2, 2):
+            transpose_inputs(e + 4)
+            copy_inputs(e + 4)
+            transpose_inputs(e + 5)
+            copy_inputs(e + 5)
+            if e == -4:
+                sort_columns("a", 0)
+                sort_columns("a", 1)
+            first_products(e + 1, 0)
+            copy_left(e + 1, 0)
+            copy_left(e + 1, 1)
             first_products(e, 1)
-            copy_left(e, 1)
-            last_product(e - 1)
-            copy_out(e - 1)
             multiply(e, 0)
             multiply(e, 1)
-            first_products(o, 0)
-            copy_left(o, 0)
-            first_products(o, 1)
-            copy_left(o, 1)
-            multiply(o, 0)
-            quantise_fused(e)
-            multiply(o, 1)
+            first_products(e + 2, 0)
+            copy_left(e + 2, 0)
+            copy_left(e + 2, 1)
+            first_products(e + 1, 1)
+            multiply(e + 1, 0)
+            multiply(e + 1, 1)
+            last_product(e - 2)
+            copy_out(e - 2)
+            last_product(e - 1)
+            copy_out(e - 1)
+            quantise_inputs((e + 4) // 2)
+            if e == -4:
+                sort_columns("b", 0)
+                sort_columns("b", 1)
+            quantise_fused(e // 2)

@@ -26,6 +26,8 @@ CHUNK_ROWS = TILES_PER_CHUNK * P
 N_CHUNKS = BATCH // CHUNK_ROWS
 N_TILES = BATCH // P
 
+DIRECT_CHUNKS = 3
+
 FLOPS = 2 * BATCH * (FEATURES * RANK + FEATURES * RANK + RANK * HIDDEN)
 
 
@@ -37,6 +39,7 @@ def tile_vnclcell_pa_t_e_kernel(
         ctx.enter_context(tc.manual_schedule())
         consts = ctx.enter_context(tc.tile_pool(name="consts", bufs=1))
         rows = ctx.enter_context(tc.tile_pool(name="rows", bufs=N_CHUNKS))
+        sorted_rows = ctx.enter_context(tc.tile_pool(name="sorted_rows", bufs=3))
         grouped_pool = ctx.enter_context(tc.tile_pool(name="grouped", bufs=3))
         operands = ctx.enter_context(tc.tile_pool(name="operands", bufs=4))
         lefts = ctx.enter_context(tc.tile_pool(name="lefts", bufs=6))
@@ -109,6 +112,17 @@ def tile_vnclcell_pa_t_e_kernel(
         for c in range(2, N_CHUNKS):
             load_rows(c)
 
+        v_sorted = {}
+
+        def sort_words(c):
+            if not DIRECT_CHUNKS <= c < N_CHUNKS:
+                return
+            v_sorted[c] = sorted_rows.tile([P, TILES_PER_CHUNK, HALF, P], I32, name="v_sorted")
+            nc.vector.tensor_copy(
+                out=v_sorted[c][:],
+                in_=v_rows[c][:].bitcast(I32).rearrange("p t (w u) -> p t u w", u=HALF),
+            )
+
         def sort_columns(w, g):
             columns = slice(g * K_PASS, (g + 1) * K_PASS)
             nc.vector.tensor_copy(
@@ -138,12 +152,19 @@ def tile_vnclcell_pa_t_e_kernel(
                 return
             c, t = divmod(i, TILES_PER_CHUNK)
             planes = banks.tile([P, 2, HALF, P], F32, name="bank")
-            for a, loaded in enumerate((v_rows[c], s_rows[c])):
-                words = loaded[:, t, :].bitcast(F32)
+            for a in range(2):
                 for u in range(HALF):
-                    nc.tensor.transpose(
-                        planes[:, a, u, :], words[:, u : FEATURES // 2 : HALF], ident[:]
-                    )
+                    if c < DIRECT_CHUNKS or a == 1:
+                        words = (v_rows[c], s_rows[c])[a][:, t, :].bitcast(F32)
+                        nc.tensor.transpose(
+                            planes[:, a, u, :], words[:, u : FEATURES // 2 : HALF], ident[:]
+                        )
+                    else:
+                        nc.tensor.transpose(
+                            planes[:, a, u, :],
+                            v_sorted[c][:, t, u, :].bitcast(F32),
+                            ident[:],
+                        )
             planes_of[i] = planes
 
         def copy_inputs(i):
@@ -241,10 +262,7 @@ def tile_vnclcell_pa_t_e_kernel(
             c, t = divmod(i, TILES_PER_CHUNK)
             if t == 0:
                 results[c] = stores.tile([P, TILES_PER_CHUNK, HIDDEN], F32, name="result")
-            if i % 4 == 3:
-                nc.vector.tensor_copy(out=results[c][:, t, :], in_=out_sums_of[i][:])
-            else:
-                nc.scalar.copy(out=results[c][:, t, :], in_=out_sums_of[i][:])
+            nc.scalar.copy(out=results[c][:, t, :], in_=out_sums_of[i][:])
             if t == TILES_PER_CHUNK - 1:
                 chunk = slice(c * CHUNK_ROWS, (c + 1) * CHUNK_ROWS)
                 nc.sync.dma_start(
@@ -253,6 +271,7 @@ def tile_vnclcell_pa_t_e_kernel(
                 )
 
         for e in range(-4, N_TILES + 2, 2):
+            sort_words((e + 6) // 2)
             transpose_inputs(e + 4)
             copy_inputs(e + 4)
             transpose_inputs(e + 5)

@@ -104,12 +104,14 @@ def tile_vnclcell_pa_t_e_kernel(
         load_scale_rows(raw_scales["b"], lambda q: Cb_scales[0, q, :])
         load_codes("b", Cb_words, 0)
         load_codes("b", Cb_words, 1)
+        load_rows(2)
+        load_rows(3)
         load_scale_rows(cc_scales, lambda q: Cc_scales[:, q, :].rearrange("g q n -> q g n"))
         nc.sync.dma_start(
             out=cc_codes[:].bitcast(I32),
             in_=Cc_words.rearrange("g p n t -> p g (n t)").bitcast(I32),
         )
-        for c in range(2, N_CHUNKS):
+        for c in range(4, N_CHUNKS):
             load_rows(c)
 
         v_sorted = {}
@@ -239,6 +241,20 @@ def tile_vnclcell_pa_t_e_kernel(
             if live(2 * c):
                 fused_codes_of[c] = quantise_pair(fused_of[c], "fused")
 
+        def quantise_fused_tile(i):
+            c, t = divmod(i, 2)
+            if t == 0:
+                fused_codes_of[c] = (
+                    operands.tile([P, 2, 2, P], U32, name="fused_codes", align_bytes=64),
+                    operands.tile([P, 2, 2, P], U8, name="fused_scales", align_bytes=64),
+                )
+            codes, scales = fused_codes_of[c]
+            nc.vector.quantize_mx(
+                out=codes[:, t].rearrange("p a b -> p (a b)").bitcast(FP8X4),
+                scales=scales[:, t].rearrange("p a b -> p (a b)"),
+                in_=fused_of[c][:, t].rearrange("p a b t -> p (a b t)"),
+            )
+
         def last_product(i):
             if not live(i):
                 return
@@ -263,12 +279,12 @@ def tile_vnclcell_pa_t_e_kernel(
             if t == 0:
                 results[c] = stores.tile([P, TILES_PER_CHUNK, HIDDEN], F32, name="result")
             nc.scalar.copy(out=results[c][:, t, :], in_=out_sums_of[i][:])
-            if t == TILES_PER_CHUNK - 1:
-                chunk = slice(c * CHUNK_ROWS, (c + 1) * CHUNK_ROWS)
-                nc.sync.dma_start(
-                    out=out[0, chunk, :].rearrange("(p t) h -> p t h", t=TILES_PER_CHUNK),
-                    in_=results[c][:],
-                )
+            chunk = slice(c * CHUNK_ROWS, (c + 1) * CHUNK_ROWS)
+            stored = out[0, chunk, :].rearrange("(p t) h -> p t h", t=TILES_PER_CHUNK)
+            if c == N_CHUNKS - 1:
+                nc.sync.dma_start(out=stored[:, t, :], in_=results[c][:, t, :])
+            elif t == TILES_PER_CHUNK - 1:
+                nc.sync.dma_start(out=stored, in_=results[c][:])
 
         for e in range(-4, N_TILES + 2, 2):
             sort_words((e + 6) // 2)
@@ -290,6 +306,8 @@ def tile_vnclcell_pa_t_e_kernel(
             copy_left(e + 2, 1)
             first_products(e + 1, 1)
             multiply(e + 1, 0)
+            if e == N_TILES - 2:
+                quantise_fused_tile(e)
             multiply(e + 1, 1)
             last_product(e - 2)
             copy_out(e - 2)
@@ -299,4 +317,7 @@ def tile_vnclcell_pa_t_e_kernel(
             if e == -4:
                 sort_columns("b", 0)
                 sort_columns("b", 1)
-            quantise_fused(e // 2)
+            if e == N_TILES - 2:
+                quantise_fused_tile(e + 1)
+            else:
+                quantise_fused(e // 2)

@@ -258,32 +258,41 @@ def tile_vnclcell_pa_t_e_kernel(
         def last_product(i):
             if not live(i):
                 return
-            codes, scales = fused_codes_of[i // 2]
-            acc = banks.tile([P, HIDDEN], F32, name="bank")
+            c, t = divmod(i, TILES_PER_CHUNK)
+            codes, scales = fused_codes_of[c]
+            if c == N_CHUNKS - 1:
+                acc = banks.tile([P, HIDDEN], F32, name="bank")
+                out_sums_of[i] = acc
+                target = acc[:]
+            else:
+                if t == 0:
+                    out_sums_of[c] = banks.tile([P, TILES_PER_CHUNK, HIDDEN], F32, name="bank")
+                target = out_sums_of[c][:, t, :]
             for g in range(R_PASSES):
                 nc.tensor.matmul_mx(
-                    out=acc[:],
-                    lhsT=codes[:, i % 2, g, :].bitcast(FP8X4),
-                    lhsT_scale=scales[:, i % 2, g, :],
+                    out=target,
+                    lhsT=codes[:, t, g, :].bitcast(FP8X4),
+                    lhsT_scale=scales[:, t, g, :],
                     rhs=cc_codes[:, g, :].bitcast(FP8X4),
                     rhs_scale=cc_scales[:, g, :],
                     start=(g == 0),
                     stop=(g == R_PASSES - 1),
                 )
-            out_sums_of[i] = acc
 
         def copy_out(i):
             if not live(i):
                 return
             c, t = divmod(i, TILES_PER_CHUNK)
-            if t == 0:
-                results[c] = stores.tile([P, TILES_PER_CHUNK, HIDDEN], F32, name="result")
-            nc.scalar.copy(out=results[c][:, t, :], in_=out_sums_of[i][:])
             chunk = slice(c * CHUNK_ROWS, (c + 1) * CHUNK_ROWS)
             stored = out[0, chunk, :].rearrange("(p t) h -> p t h", t=TILES_PER_CHUNK)
             if c == N_CHUNKS - 1:
+                if t == 0:
+                    results[c] = stores.tile([P, TILES_PER_CHUNK, HIDDEN], F32, name="result")
+                nc.scalar.copy(out=results[c][:, t, :], in_=out_sums_of[i][:])
                 nc.sync.dma_start(out=stored[:, t, :], in_=results[c][:, t, :])
             elif t == TILES_PER_CHUNK - 1:
+                results[c] = stores.tile([P, TILES_PER_CHUNK, HIDDEN], F32, name="result")
+                nc.scalar.copy(out=results[c][:], in_=out_sums_of[c][:])
                 nc.sync.dma_start(out=stored, in_=results[c][:])
 
         for e in range(-4, N_TILES + 2, 2):

@@ -26,6 +26,9 @@ CHUNK_ROWS = TILES_PER_CHUNK * P
 N_CHUNKS = BATCH // CHUNK_ROWS
 N_TILES = BATCH // P
 
+T_PER_BANK = 2
+RUN = 4
+
 DIRECT_CHUNKS = 3
 
 FLOPS = 2 * BATCH * (FEATURES * RANK + FEATURES * RANK + RANK * HIDDEN)
@@ -42,7 +45,7 @@ def tile_vnclcell_pa_t_e_kernel(
         sorted_rows = ctx.enter_context(tc.tile_pool(name="sorted_rows", bufs=3))
         grouped_pool = ctx.enter_context(tc.tile_pool(name="grouped", bufs=3))
         operands = ctx.enter_context(tc.tile_pool(name="operands", bufs=4))
-        lefts = ctx.enter_context(tc.tile_pool(name="lefts", bufs=6))
+        lefts = ctx.enter_context(tc.tile_pool(name="lefts", bufs=4))
         stores = ctx.enter_context(tc.tile_pool(name="stores", bufs=4))
         banks = ctx.enter_context(tc.psum_pool(name="banks", bufs=8))
 
@@ -140,6 +143,7 @@ def tile_vnclcell_pa_t_e_kernel(
         grouped_of = {}
         inputs_of = {}
         sums_of = {}
+        s_sums_of = {}
         left_of = {}
         fused_of = {}
         fused_codes_of = {}
@@ -175,10 +179,10 @@ def tile_vnclcell_pa_t_e_kernel(
             c, t = divmod(i, 2)
             if t == 0:
                 grouped_of[c] = grouped_pool.tile(
-                    [P, 2, 2, P, PACK], BF16, name="in_grouped", align_bytes=64
+                    [P, 2, TILES_PER_CHUNK, P, PACK], BF16, name="in_grouped", align_bytes=64
                 )
             nc.scalar.copy(
-                out=grouped_of[c][:, t].bitcast(F32),
+                out=grouped_of[c][:, :, t].bitcast(F32),
                 in_=planes_of[i][:].rearrange("p a u b -> p a b u"),
             )
 
@@ -196,31 +200,54 @@ def tile_vnclcell_pa_t_e_kernel(
             if live(2 * c):
                 inputs_of[c] = quantise_pair(grouped_of[c], "in")
 
-        def first_products(i, a):
+        def multiply_v(c, g):
+            if not live(2 * c):
+                return
+            codes, scales = inputs_of[c]
+            for pair in range(PACK // T_PER_BANK):
+                sums = banks.tile([P, T_PER_BANK, CHUNK_ROWS], F32, name="bank")
+                for j in range(T_PER_BANK):
+                    t = pair * T_PER_BANK + j
+                    nc.tensor.matmul_mx(
+                        out=sums[:, j, :],
+                        lhsT=sorted_codes["a"][:, g, t, :].bitcast(FP8X4),
+                        lhsT_scale=sorted_scales["a"][:, g, t, :],
+                        rhs=codes[:, 0].rearrange("p i b -> p (i b)").bitcast(FP8X4),
+                        rhs_scale=scales[:, 0].rearrange("p i b -> p (i b)"),
+                        start=True,
+                        stop=True,
+                    )
+                sums_of[(c, g, pair)] = sums
+
+        def multiply_s(i):
             if not live(i):
                 return
-            codes, scales = inputs_of[i // 2]
-            w = "ab"[a]
+            c, tile = divmod(i, TILES_PER_CHUNK)
+            codes, scales = inputs_of[c]
             for g in range(R_PASSES):
                 sums = banks.tile([P, PACK, P], F32, name="bank")
                 for t in range(PACK):
                     nc.tensor.matmul_mx(
                         out=sums[:, t, :],
-                        lhsT=sorted_codes[w][:, g, t, :].bitcast(FP8X4),
-                        lhsT_scale=sorted_scales[w][:, g, t, :],
-                        rhs=codes[:, i % 2, a, :].bitcast(FP8X4),
-                        rhs_scale=scales[:, i % 2, a, :],
+                        lhsT=sorted_codes["b"][:, g, t, :].bitcast(FP8X4),
+                        lhsT_scale=sorted_scales["b"][:, g, t, :],
+                        rhs=codes[:, 1, tile, :].bitcast(FP8X4),
+                        rhs_scale=scales[:, 1, tile, :],
                         start=True,
                         stop=True,
                     )
-                sums_of[(i, g, w)] = sums
+                s_sums_of[(i, g)] = sums
 
-        def copy_left(i, g):
-            if not live(i):
+        def copy_left(c, g):
+            if not live(2 * c):
                 return
-            left = lefts.tile([P, P, PACK], F32, name="left")
-            nc.scalar.copy(out=left[:], in_=sums_of[(i, g, "a")][:].rearrange("p t b -> p b t"))
-            left_of[(i, g)] = left
+            left = lefts.tile([P, PACK, CHUNK_ROWS], F32, name="left")
+            for pair in range(PACK // T_PER_BANK):
+                nc.scalar.copy(
+                    out=left[:, pair * T_PER_BANK : (pair + 1) * T_PER_BANK, :],
+                    in_=sums_of[(c, g, pair)][:],
+                )
+            left_of[(c, g)] = left
 
         def multiply(i, g):
             if not live(i):
@@ -231,9 +258,11 @@ def tile_vnclcell_pa_t_e_kernel(
                     [P, 2, R_PASSES, P, PACK], BF16, name="fused_grouped", align_bytes=64
                 )
             nc.vector.tensor_tensor(
-                out=fused_of[c][:, t, g],
-                in0=sums_of[(i, g, "b")][:].rearrange("p t b -> p b t"),
-                in1=left_of[(i, g)][:],
+                out=fused_of[c][:, t, g].rearrange("p (b i) t -> p b t i", i=RUN),
+                in0=s_sums_of[(i, g)][:].rearrange("p t (b i) -> p b t i", i=RUN),
+                in1=left_of[(c, g)][:, :, t * P : (t + 1) * P].rearrange(
+                    "p t (b i) -> p b t i", i=RUN
+                ),
                 op=mybir.AluOpType.mult,
             )
 
@@ -304,20 +333,18 @@ def tile_vnclcell_pa_t_e_kernel(
             if e == -4:
                 sort_columns("a", 0)
                 sort_columns("a", 1)
-            first_products(e + 1, 0)
-            copy_left(e + 1, 0)
-            copy_left(e + 1, 1)
-            first_products(e, 1)
+            multiply_s(e)
             multiply(e, 0)
             multiply(e, 1)
-            first_products(e + 2, 0)
-            copy_left(e + 2, 0)
-            copy_left(e + 2, 1)
-            first_products(e + 1, 1)
+            multiply_v(e // 2 + 1, 0)
+            copy_left(e // 2 + 1, 0)
+            multiply_s(e + 1)
             multiply(e + 1, 0)
             if e == N_TILES - 2:
                 quantise_fused_tile(e)
             multiply(e + 1, 1)
+            multiply_v(e // 2 + 1, 1)
+            copy_left(e // 2 + 1, 1)
             last_product(e - 2)
             copy_out(e - 2)
             last_product(e - 1)

@@ -142,7 +142,6 @@ def tile_vnclcell_pa_t_e_kernel(
         planes_of = {}
         grouped_of = {}
         inputs_of = {}
-        sums_of = {}
         s_sums_of = {}
         left_of = {}
         fused_of = {}
@@ -200,54 +199,45 @@ def tile_vnclcell_pa_t_e_kernel(
             if live(2 * c):
                 inputs_of[c] = quantise_pair(grouped_of[c], "in")
 
-        def multiply_v(c, g):
+        def multiply_v(c, g, pair):
             if not live(2 * c):
                 return
             codes, scales = inputs_of[c]
-            for pair in range(PACK // T_PER_BANK):
-                sums = banks.tile([P, T_PER_BANK, CHUNK_ROWS], F32, name="bank")
-                for j in range(T_PER_BANK):
-                    t = pair * T_PER_BANK + j
-                    nc.tensor.matmul_mx(
-                        out=sums[:, j, :],
-                        lhsT=sorted_codes["a"][:, g, t, :].bitcast(FP8X4),
-                        lhsT_scale=sorted_scales["a"][:, g, t, :],
-                        rhs=codes[:, 0].rearrange("p i b -> p (i b)").bitcast(FP8X4),
-                        rhs_scale=scales[:, 0].rearrange("p i b -> p (i b)"),
-                        start=True,
-                        stop=True,
-                    )
-                sums_of[(c, g, pair)] = sums
+            if pair == 0:
+                left_of[(c, g)] = lefts.tile([P, PACK, CHUNK_ROWS], F32, name="left")
+            sums = banks.tile([P, T_PER_BANK, CHUNK_ROWS], F32, name="bank")
+            for j in range(T_PER_BANK):
+                t = pair * T_PER_BANK + j
+                nc.tensor.matmul_mx(
+                    out=sums[:, j, :],
+                    lhsT=sorted_codes["a"][:, g, t, :].bitcast(FP8X4),
+                    lhsT_scale=sorted_scales["a"][:, g, t, :],
+                    rhs=codes[:, 0].rearrange("p i b -> p (i b)").bitcast(FP8X4),
+                    rhs_scale=scales[:, 0].rearrange("p i b -> p (i b)"),
+                    start=True,
+                    stop=True,
+                )
+            nc.scalar.copy(
+                out=left_of[(c, g)][:, pair * T_PER_BANK : (pair + 1) * T_PER_BANK, :], in_=sums[:]
+            )
 
-        def multiply_s(i):
+        def multiply_s(i, g):
             if not live(i):
                 return
             c, tile = divmod(i, TILES_PER_CHUNK)
             codes, scales = inputs_of[c]
-            for g in range(R_PASSES):
-                sums = banks.tile([P, PACK, P], F32, name="bank")
-                for t in range(PACK):
-                    nc.tensor.matmul_mx(
-                        out=sums[:, t, :],
-                        lhsT=sorted_codes["b"][:, g, t, :].bitcast(FP8X4),
-                        lhsT_scale=sorted_scales["b"][:, g, t, :],
-                        rhs=codes[:, 1, tile, :].bitcast(FP8X4),
-                        rhs_scale=scales[:, 1, tile, :],
-                        start=True,
-                        stop=True,
-                    )
-                s_sums_of[(i, g)] = sums
-
-        def copy_left(c, g):
-            if not live(2 * c):
-                return
-            left = lefts.tile([P, PACK, CHUNK_ROWS], F32, name="left")
-            for pair in range(PACK // T_PER_BANK):
-                nc.scalar.copy(
-                    out=left[:, pair * T_PER_BANK : (pair + 1) * T_PER_BANK, :],
-                    in_=sums_of[(c, g, pair)][:],
+            sums = banks.tile([P, PACK, P], F32, name="bank")
+            for t in range(PACK):
+                nc.tensor.matmul_mx(
+                    out=sums[:, t, :],
+                    lhsT=sorted_codes["b"][:, g, t, :].bitcast(FP8X4),
+                    lhsT_scale=sorted_scales["b"][:, g, t, :],
+                    rhs=codes[:, 1, tile, :].bitcast(FP8X4),
+                    rhs_scale=scales[:, 1, tile, :],
+                    start=True,
+                    stop=True,
                 )
-            left_of[(c, g)] = left
+            s_sums_of[(i, g)] = sums
 
         def multiply(i, g):
             if not live(i):
@@ -326,6 +316,8 @@ def tile_vnclcell_pa_t_e_kernel(
 
         for e in range(-4, N_TILES + 2, 2):
             sort_words((e + 6) // 2)
+            multiply_s(e, 0)
+            multiply(e, 0)
             transpose_inputs(e + 4)
             copy_inputs(e + 4)
             transpose_inputs(e + 5)
@@ -333,18 +325,18 @@ def tile_vnclcell_pa_t_e_kernel(
             if e == -4:
                 sort_columns("a", 0)
                 sort_columns("a", 1)
-            multiply_s(e)
-            multiply(e, 0)
+            multiply_s(e, 1)
             multiply(e, 1)
-            multiply_v(e // 2 + 1, 0)
-            copy_left(e // 2 + 1, 0)
-            multiply_s(e + 1)
+            multiply_v(e // 2 + 1, 0, 0)
+            multiply_s(e + 1, 0)
             multiply(e + 1, 0)
+            multiply_v(e // 2 + 1, 0, 1)
+            multiply_s(e + 1, 1)
             if e == N_TILES - 2:
                 quantise_fused_tile(e)
             multiply(e + 1, 1)
-            multiply_v(e // 2 + 1, 1)
-            copy_left(e // 2 + 1, 1)
+            multiply_v(e // 2 + 1, 1, 0)
+            multiply_v(e // 2 + 1, 1, 1)
             last_product(e - 2)
             copy_out(e - 2)
             last_product(e - 1)

@@ -119,8 +119,11 @@ def tile_vnclcell_pa_t_e_kernel(
 
         v_sorted = {}
 
+        def is_sorted(c):
+            return DIRECT_CHUNKS <= c < N_CHUNKS and c % 3 != 0
+
         def sort_words(c):
-            if not DIRECT_CHUNKS <= c < N_CHUNKS:
+            if not is_sorted(c):
                 return
             v_sorted[c] = sorted_rows.tile([P, TILES_PER_CHUNK, HALF, P], I32, name="v_sorted")
             nc.vector.tensor_copy(
@@ -159,7 +162,7 @@ def tile_vnclcell_pa_t_e_kernel(
             planes = banks.tile([P, 2, HALF, P], F32, name="bank")
             for a in range(2):
                 for u in range(HALF):
-                    if c < DIRECT_CHUNKS or a == 1:
+                    if a == 1 or not is_sorted(c):
                         words = (v_rows[c], s_rows[c])[a][:, t, :].bitcast(F32)
                         nc.tensor.transpose(
                             planes[:, a, u, :], words[:, u : FEATURES // 2 : HALF], ident[:]

from contextlib import ExitStack

import concourse.mybir as mybir
from concourse.masks import make_identity

BF16 = mybir.dt.bfloat16
F32 = mybir.dt.float32
I32 = mybir.dt.int32
U32 = mybir.dt.uint32
U8 = mybir.dt.uint8
FP8X4 = mybir.dt.float8_e4m3fn_x4

P = 128
PACK = 4
K_PASS = P * PACK
HALF = 2

BATCH = 4096
FEATURES = 512
RANK = 1024
HIDDEN = 256
R_PASSES = RANK // K_PASS

TILES_PER_CHUNK = 2
CHUNK_ROWS = TILES_PER_CHUNK * P
N_CHUNKS = BATCH // CHUNK_ROWS
N_TILES = BATCH // P

T_PER_BANK = 2
RUN = 4

DIRECT_CHUNKS = 3

FLOPS = 2 * BATCH * (FEATURES * RANK + FEATURES * RANK + RANK * HIDDEN)


def tile_vnclcell_pa_t_e_kernel(
    tc, v, s, Ca_words, Ca_scales, Cb_words, Cb_scales, Cc_words, Cc_scales, out
):
    nc = tc.nc
    with ExitStack() as ctx:
        ctx.enter_context(tc.manual_schedule())
        consts = ctx.enter_context(tc.tile_pool(name="consts", bufs=1))
        rows = ctx.enter_context(tc.tile_pool(name="rows", bufs=N_CHUNKS))
        sorted_rows = ctx.enter_context(tc.tile_pool(name="sorted_rows", bufs=3))
        grouped_pool = ctx.enter_context(tc.tile_pool(name="grouped", bufs=3))
        operands = ctx.enter_context(tc.tile_pool(name="operands", bufs=4))
        lefts = ctx.enter_context(tc.tile_pool(name="lefts", bufs=4))
        stores = ctx.enter_context(tc.tile_pool(name="stores", bufs=4))
        banks = ctx.enter_context(tc.psum_pool(name="banks", bufs=8))

        ident = consts.tile([P, P], F32, name="ident")
        make_identity(nc, ident[:])

        raw_codes = {}
        raw_scales = {}
        sorted_codes = {}
        sorted_scales = {}
        for w in ("a", "b"):
            raw_codes[w] = consts.tile([P, RANK], U32, name="raw_codes_" + w, align_bytes=64)
            raw_scales[w] = consts.tile([P, RANK], U8, name="raw_scales_" + w, align_bytes=64)
            sorted_codes[w] = consts.tile(
                [P, R_PASSES, PACK, P], U32, name="sorted_codes_" + w, align_bytes=64
            )
            sorted_scales[w] = consts.tile(
                [P, R_PASSES, PACK, P], U8, name="sorted_scales_" + w, align_bytes=64
            )
        cc_codes = consts.tile([P, R_PASSES, HIDDEN], U32, name="cc_codes", align_bytes=64)
        cc_scales = consts.tile([P, R_PASSES, HIDDEN], U8, name="cc_scales", align_bytes=64)
        nc.vector.memset(raw_scales["a"][:].bitcast(I32), 0)
        nc.vector.memset(raw_scales["b"][:].bitcast(I32), 0)
        nc.vector.memset(cc_scales[:].bitcast(I32), 0)

        v_rows = []
        s_rows = []

        def load_rows(c):
            chunk = slice(c * CHUNK_ROWS, (c + 1) * CHUNK_ROWS)
            for source, kept, name in ((v, v_rows, "v_rows"), (s, s_rows, "s_rows")):
                loaded = rows.tile([P, TILES_PER_CHUNK, FEATURES], BF16, name=name)
                nc.sync.dma_start(
                    out=loaded[:],
                    in_=source[chunk, :].rearrange("(p t) k -> p t k", t=TILES_PER_CHUNK),
                )
                kept.append(loaded)

        def load_scale_rows(plane, dram_rows_of_quadrant):
            for quadrant in range(4):
                nc.sync.dma_start(
                    out=plane[32 * quadrant : 32 * quadrant + 4].bitcast(I32),
                    in_=dram_rows_of_quadrant(slice(4 * quadrant, 4 * quadrant + 4)).bitcast(I32),
                )

        def load_codes(w, words, g):
            nc.sync.dma_start(
                out=raw_codes[w][:, g * K_PASS : (g + 1) * K_PASS].bitcast(I32),
                in_=words[0]
                .rearrange("p n t -> p (n t)")[:, g * K_PASS * PACK : (g + 1) * K_PASS * PACK]
                .bitcast(I32),
            )

        load_rows(0)
        load_scale_rows(raw_scales["a"], lambda q: Ca_scales[0, q, :])
        load_codes("a", Ca_words, 0)
        load_codes("a", Ca_words, 1)
        load_rows(1)
        load_scale_rows(raw_scales["b"], lambda q: Cb_scales[0, q, :])
        load_codes("b", Cb_words, 0)
        load_codes("b", Cb_words, 1)
        load_rows(2)
        load_rows(3)
        load_scale_rows(cc_scales, lambda q: Cc_scales[:, q, :].rearrange("g q n -> q g n"))
        nc.sync.dma_start(
            out=cc_codes[:].bitcast(I32),
            in_=Cc_words.rearrange("g p n t -> p g (n t)").bitcast(I32),
        )
        for c in range(4, N_CHUNKS):
            load_rows(c)

        v_sorted = {}

        def is_sorted(c):
            return DIRECT_CHUNKS <= c < N_CHUNKS and c % 3 != 0

        def sort_words(c):
            if not is_sorted(c):
                return
            v_sorted[c] = sorted_rows.tile([P, TILES_PER_CHUNK, HALF, P], I32, name="v_sorted")
            nc.vector.tensor_copy(
                out=v_sorted[c][:],
                in_=v_rows[c][:].bitcast(I32).rearrange("p t (w u) -> p t u w", u=HALF),
            )

        def sort_columns(w, g):
            columns = slice(g * K_PASS, (g + 1) * K_PASS)
            nc.vector.tensor_copy(
                out=sorted_codes[w][:, g].bitcast(I32),
                in_=raw_codes[w][:, columns].bitcast(I32).rearrange("p (m t) -> p t m", t=PACK),
            )
            nc.vector.tensor_copy(
                out=sorted_scales[w][:, g],
                in_=raw_scales[w][:, columns].rearrange("p (m t) -> p t m", t=PACK),
            )

        planes_of = {}
        grouped_of = {}
        inputs_of = {}
        s_sums_of = {}
        left_of = {}
        fused_of = {}
        fused_codes_of = {}
        out_sums_of = {}
        results = {}

        def live(i):
            return 0 <= i < N_TILES

        def transpose_inputs(i):
            if not live(i):
                return
            c, t = divmod(i, TILES_PER_CHUNK)
            planes = banks.tile([P, 2, HALF, P], F32, name="bank")
            for a in range(2):
                for u in range(HALF):
                    if a == 1 or not is_sorted(c):
                        words = (v_rows[c], s_rows[c])[a][:, t, :].bitcast(F32)
                        nc.tensor.transpose(
                            planes[:, a, u, :], words[:, u : FEATURES // 2 : HALF], ident[:]
                        )
                    else:
                        nc.tensor.transpose(
                            planes[:, a, u, :],
                            v_sorted[c][:, t, u, :].bitcast(F32),
                            ident[:],
                        )
            planes_of[i] = planes

        def copy_inputs(i):
            if not live(i):
                return
            c, t = divmod(i, 2)
            if t == 0:
                grouped_of[c] = grouped_pool.tile(
                    [P, 2, TILES_PER_CHUNK, P, PACK], BF16, name="in_grouped", align_bytes=64
                )
            nc.scalar.copy(
                out=grouped_of[c][:, :, t].bitcast(F32),
                in_=planes_of[i][:].rearrange("p a u b -> p a b u"),
            )

        def quantise_pair(grouped, name):
            codes = operands.tile([P, 2, 2, P], U32, name=name + "_codes", align_bytes=64)
            scales = operands.tile([P, 2, 2, P], U8, name=name + "_scales", align_bytes=64)
            nc.vector.quantize_mx(
                out=codes[:].rearrange("p i a b -> p (i a b)").bitcast(FP8X4),
                scales=scales[:].rearrange("p i a b -> p (i a b)"),
                in_=grouped[:].rearrange("p i a b t -> p (i a b t)"),
            )
            return codes, scales

        def quantise_inputs(c):
            if live(2 * c):
                inputs_of[c] = quantise_pair(grouped_of[c], "in")

        def multiply_v(c, g, pair):
            if not live(2 * c):
                return
            codes, scales = inputs_of[c]
            if pair == 0:
                left_of[(c, g)] = lefts.tile([P, PACK, CHUNK_ROWS], F32, name="left")
            sums = banks.tile([P, T_PER_BANK, CHUNK_ROWS], F32, name="bank")
            for j in range(T_PER_BANK):
                t = pair * T_PER_BANK + j
                nc.tensor.matmul_mx(
                    out=sums[:, j, :],
                    lhsT=sorted_codes["a"][:, g, t, :].bitcast(FP8X4),
                    lhsT_scale=sorted_scales["a"][:, g, t, :],
                    rhs=codes[:, 0].rearrange("p i b -> p (i b)").bitcast(FP8X4),
                    rhs_scale=scales[:, 0].rearrange("p i b -> p (i b)"),
                    start=True,
                    stop=True,
                )
            nc.scalar.copy(
                out=left_of[(c, g)][:, pair * T_PER_BANK : (pair + 1) * T_PER_BANK, :], in_=sums[:]
            )

        def multiply_s(i, g):
            if not live(i):
                return
            c, tile = divmod(i, TILES_PER_CHUNK)
            codes, scales = inputs_of[c]
            sums = banks.tile([P, PACK, P], F32, name="bank")
            for t in range(PACK):
                nc.tensor.matmul_mx(
                    out=sums[:, t, :],
                    lhsT=sorted_codes["b"][:, g, t, :].bitcast(FP8X4),
                    lhsT_scale=sorted_scales["b"][:, g, t, :],
                    rhs=codes[:, 1, tile, :].bitcast(FP8X4),
                    rhs_scale=scales[:, 1, tile, :],
                    start=True,
                    stop=True,
                )
            s_sums_of[(i, g)] = sums

        def multiply(i, g):
            if not live(i):
                return
            c, t = divmod(i, 2)
            if t == 0 and g == 0:
                fused_of[c] = grouped_pool.tile(
                    [P, 2, R_PASSES, P, PACK], BF16, name="fused_grouped", align_bytes=64
                )
            nc.vector.tensor_tensor(
                out=fused_of[c][:, t, g].rearrange("p (b i) t -> p b t i", i=RUN),
                in0=s_sums_of[(i, g)][:].rearrange("p t (b i) -> p b t i", i=RUN),
                in1=left_of[(c, g)][:, :, t * P : (t + 1) * P].rearrange(
                    "p t (b i) -> p b t i", i=RUN
                ),
                op=mybir.AluOpType.mult,
            )

        def quantise_fused(c):
            if live(2 * c):
                fused_codes_of[c] = quantise_pair(fused_of[c], "fused")

        def quantise_fused_tile(i):
            c, t = divmod(i, 2)
            if t == 0:
                fused_codes_of[c] = (
                    operands.tile([P, 2, 2, P], U32, name="fused_codes", align_bytes=64),
                    operands.tile([P, 2, 2, P], U8, name="fused_scales", align_bytes=64),
                )
            codes, scales = fused_codes_of[c]
            nc.vector.quantize_mx(
                out=codes[:, t].rearrange("p a b -> p (a b)").bitcast(FP8X4),
                scales=scales[:, t].rearrange("p a b -> p (a b)"),
                in_=fused_of[c][:, t].rearrange("p a b t -> p (a b t)"),
            )

        def last_product(i):
            if not live(i):
                return
            c, t = divmod(i, TILES_PER_CHUNK)
            codes, scales = fused_codes_of[c]
            if c == N_CHUNKS - 1:
                acc = banks.tile([P, HIDDEN], F32, name="bank")
                out_sums_of[i] = acc
                target = acc[:]
            else:
                if t == 0:
                    out_sums_of[c] = banks.tile([P, TILES_PER_CHUNK, HIDDEN], F32, name="bank")
                target = out_sums_of[c][:, t, :]
            for g in range(R_PASSES):
                nc.tensor.matmul_mx(
                    out=target,
                    lhsT=codes[:, t, g, :].bitcast(FP8X4),
                    lhsT_scale=scales[:, t, g, :],
                    rhs=cc_codes[:, g, :].bitcast(FP8X4),
                    rhs_scale=cc_scales[:, g, :],
                    start=(g == 0),
                    stop=(g == R_PASSES - 1),
                )

        def copy_out(i):
            if not live(i):
                return
            c, t = divmod(i, TILES_PER_CHUNK)
            chunk = slice(c * CHUNK_ROWS, (c + 1) * CHUNK_ROWS)
            stored = out[0, chunk, :].rearrange("(p t) h -> p t h", t=TILES_PER_CHUNK)
            if c == N_CHUNKS - 1:
                if t == 0:
                    results[c] = stores.tile([P, TILES_PER_CHUNK, HIDDEN], F32, name="result")
                nc.scalar.copy(out=results[c][:, t, :], in_=out_sums_of[i][:])
                nc.sync.dma_start(out=stored[:, t, :], in_=results[c][:, t, :])
            elif t == TILES_PER_CHUNK - 1:
                results[c] = stores.tile([P, TILES_PER_CHUNK, HIDDEN], F32, name="result")
                nc.scalar.copy(out=results[c][:], in_=out_sums_of[c][:])
                nc.sync.dma_start(out=stored, in_=results[c][:])

        for e in range(-4, N_TILES + 2, 2):
            sort_words((e + 6) // 2)
            multiply_s(e, 0)
            multiply(e, 0)
            transpose_inputs(e + 4)
            copy_inputs(e + 4)
            transpose_inputs(e + 5)
            copy_inputs(e + 5)
            if e == -4:
                sort_columns("a", 0)
                sort_columns("a", 1)
            multiply_s(e, 1)
            multiply(e, 1)
            multiply_v(e // 2 + 1, 0, 0)
            multiply_s(e + 1, 0)
            multiply(e + 1, 0)
            multiply_v(e // 2 + 1, 0, 1)
            multiply_s(e + 1, 1)
            if e == N_TILES - 2:
                quantise_fused_tile(e)
            multiply(e + 1, 1)
            multiply_v(e // 2 + 1, 1, 0)
            multiply_v(e // 2 + 1, 1, 1)
            last_product(e - 2)
            copy_out(e - 2)
            last_product(e - 1)
            copy_out(e - 1)
            quantise_inputs((e + 4) // 2)
            if e == -4:
                sort_columns("b", 0)
                sort_columns("b", 1)
            if e == N_TILES - 2:
                quantise_fused_tile(e + 1)
            else:
                quantise_fused(e // 2)
